import numpy as np
import ml_dtypes


def mxq(x, axis, fmt="e4m3"):
    dtype, down = {"e4m3": (ml_dtypes.float8_e4m3fn, 7), "e5m2": (ml_dtypes.float8_e5m2, 14)}[fmt]
    v = np.moveaxis(np.asarray(x, np.float32).astype(ml_dtypes.bfloat16).astype(np.float64), axis, -1)
    blocks = v.reshape(v.shape[:-1] + (-1, 32))
    amax = np.abs(blocks).max(-1, keepdims=True)
    byte = np.maximum(np.where(amax > 0, np.frexp(amax)[1] - 1 + 127, 0) - down, 1)
    scale = np.exp2(byte - 127.0)
    codes = (blocks / scale).astype(np.float32).astype(dtype).astype(np.float64)
    return np.moveaxis((codes * scale).reshape(v.shape), -1, axis)


WIDE = False


def mx_kscale(k):
    if not WIDE:
        return np.ones(k)
    levels = np.array([10, -10, 5, -5, 0])
    a = np.random.permutation(np.resize(levels, k // 512 * 4)).reshape(k // 512, 4)
    idx = np.arange(k)
    return np.exp2(a[idx // 512, idx % 128 // 32])


BF16 = ml_dtypes.bfloat16


def bf(x):
    return np.asarray(x, np.float32).astype(BF16)


def f64(x):
    return np.asarray(x).astype(np.float64)


B, N, D, BD = 2, 512, 2048, 512


def setup_inputs():
    s, u = mx_kscale(D), mx_kscale(D)
    t = mx_kscale(BD)
    return {
        "keys": bf(np.random.standard_normal((B, N, D)) * s),
        "values": bf(np.random.standard_normal((B, N, D)) * u),
        "Wbk": bf(np.random.standard_normal((BD, D)) / np.sqrt(D) / s[None, :]),
        "bbk": bf(np.random.standard_normal(BD) * 0.1),
        "Wbv": bf(np.random.standard_normal((BD, D)) / np.sqrt(D) / u[None, :] * t[:, None]),
        "bbv": bf(np.random.standard_normal(BD) * 0.1 * t),
        "Wbc": bf(np.random.standard_normal((D, BD)) / np.sqrt(BD) / t[None, :]),
        "bbc": bf(np.random.standard_normal(D) * 0.1),
    }


def reference(keys, values, Wbk, bbk, Wbv, bbv, Wbc, bbc):
    k = (mxq(f64(keys), 2, "e4m3") @ mxq(f64(Wbk), 1, "e4m3").T) + f64(bbk)
    v = (mxq(f64(values), 2, "e4m3") @ mxq(f64(Wbv), 1, "e4m3").T) + f64(bbv)
    return (mxq(k * v, 2, "e4m3") @ mxq(f64(Wbc), 1, "e4m3").T) + f64(bbc)

@@ -1,0 +1,229 @@
+import concourse.mybir as mybir
+from concourse.masks import make_identity
+
+F32 = mybir.dt.float32
+BF16 = mybir.dt.bfloat16
+U32 = mybir.dt.uint32
+U8 = mybir.dt.uint8
+FP8X4 = mybir.dt.float8_e4m3fn_x4
+ADD = mybir.AluOpType.add
+MULT = mybir.AluOpType.mult
+IDENTITY = mybir.ActivationFunctionType.Identity
+
+P = 128
+TOKENS = 1024
+D = 2048
+BD = 512
+K_PASS = 512
+PASSES = D // K_PASS
+BANK = 512
+BLOCK = 256
+BLOCKS = TOKENS // BLOCK
+SLAB = 4096
+SLAB_BANKS = 4
+RAW_BUFS = 8
+
+FLOPS = 2 * TOKENS * (D * BD + D * BD + BD * D)
+
+
+def tile_learnedbindingmemory_pa_kernel(tc, keys, values, Wbk, bbk, Wbv, bbv, Wbc, bbc, out):
+    nc = tc.nc
+    source = {
+        "keys": keys.flatten_outer_dims(),
+        "values": values.flatten_outer_dims(),
+        "Wbk": Wbk,
+        "Wbv": Wbv,
+        "Wbc": Wbc,
+    }
+    out_rows = out.flatten_outer_dims().rearrange("(i p m) d -> i p m d", p=P, m=2)
+
+    load_order = [("Wbk", 0), ("Wbk", 1), ("Wbv", 0), ("Wbv", 1), ("keys", 0), ("values", 0), ("Wbc", 0), ("Wbc", 1)]
+    for i in range(1, BLOCKS):
+        load_order.extend([("keys", i), ("values", i)])
+
+    with tc.tile_pool(name="const", bufs=1) as const, tc.tile_pool(name="raw", bufs=RAW_BUFS) as raw_pool, tc.tile_pool(
+        name="grouped", bufs=3
+    ) as grouped_pool, tc.tile_pool(name="weights", bufs=1) as weight_pool, tc.tile_pool(
+        name="stream", bufs=3
+    ) as stream_pool, tc.tile_pool(name="bind", bufs=2) as bind_pool, tc.tile_pool(
+        name="result", bufs=4
+    ) as result_pool, tc.psum_pool(name="psum", bufs=8) as psum:
+        words = {}
+        grouped = {}
+        codes = {}
+        scales = {}
+
+        def load(slab):
+            name, index = slab
+            raw = raw_pool.tile([P, SLAB], BF16)
+            if name == "Wbc":
+                rows = source[name][1024 * index : 1024 * (index + 1), :]
+                nc.sync.dma_start(
+                    out=raw[:].rearrange("p (c k) -> p c k", c=8), in_=rows.rearrange("(c p) k -> p c k", p=P)
+                )
+                words[slab] = raw[:].bitcast(F32).rearrange("p (j c u w) -> p j u c w", j=SLAB_BANKS, c=2, u=2)
+            else:
+                rows = source[name][256 * index : 256 * (index + 1), :]
+                nc.sync.dma_start(out=raw[:], in_=rows.rearrange("(p c) d -> p (c d)", c=2))
+                words[slab] = raw[:].bitcast(F32).rearrange("p (c g u w) -> p g u c w", c=2, g=PASSES, u=2)
+
+        def turn(slab):
+            turned = grouped_pool.tile([P, SLAB], BF16, align_bytes=64)
+            turned_words = turned[:].bitcast(F32)
+            for j in range(SLAB_BANKS):
+                bank = psum.tile([P, BANK], F32, tag="bank")
+                for u in range(2):
+                    for c in range(2):
+                        nc.tensor.transpose(bank[:, (2 * u + c) * P : (2 * u + c + 1) * P], words[slab][:, j, u, c, :], ident[:])
+                pairs_in = bank[:].rearrange("p (u r) -> p r u", u=2)
+                pairs_out = turned_words[:, BANK * j : BANK * (j + 1)].rearrange("p (r u) -> p r u", u=2)
+                if slab[0] in ("Wbk", "Wbv", "Wbc") and j == SLAB_BANKS - 1:
+                    nc.vector.tensor_copy(out=pairs_out, in_=pairs_in)
+                else:
+                    nc.scalar.copy(out=pairs_out, in_=pairs_in)
+            grouped[slab] = turned
+            following = load_order.index(slab) + RAW_BUFS
+            if following < len(load_order):
+                load(load_order[following])
+
+        def quantise(slab):
+            pool = weight_pool if slab[0] in ("Wbk", "Wbv", "Wbc") else stream_pool
+            label = "%s%d" % slab if pool is weight_pool else "stream"
+            slab_codes = pool.tile([P, SLAB // 4], U32, align_bytes=64, name="codes_" + label)
+            slab_scales = pool.tile([P, SLAB // 4], U8, align_bytes=64, name="scales_" + label)
+            nc.vector.quantize_mx(out=slab_codes[:].bitcast(FP8X4), scales=slab_scales[:], in_=grouped[slab][:])
+            codes[slab] = slab_codes
+            scales[slab] = slab_scales
+
+        def project(weight, stream, u):
+            bank = psum.tile([P, BANK], F32, tag="bank")
+            for e in range(2):
+                for g in range(PASSES):
+                    w_cols = slice(BLOCK * g + P * e, BLOCK * g + P * (e + 1))
+                    s_cols = slice(BLOCK * g, BLOCK * (g + 1))
+                    nc.tensor.matmul_mx(
+                        out=bank[:, BLOCK * e : BLOCK * (e + 1)],
+                        lhsT=codes[(weight, u)][:, w_cols].bitcast(FP8X4),
+                        lhsT_scale=scales[(weight, u)][:, w_cols],
+                        rhs=codes[stream][:, s_cols].bitcast(FP8X4),
+                        rhs_scale=scales[stream][:, s_cols],
+                        start=(g == 0),
+                        stop=(g == PASSES - 1),
+                    )
+            return bank
+
+        k_of = {}
+        bound_codes = {}
+        bound_scales = {}
+
+        def project_keys(i):
+            k_sb = bind_pool.tile([P, 4, BLOCK], F32)
+            for u in range(2):
+                bank = project("Wbk", ("keys", i), u)
+                for e in range(2):
+                    t = 2 * u + e
+                    nc.scalar.activation(
+                        out=k_sb[:, t, :], in_=bank[:, BLOCK * e : BLOCK * (e + 1)], func=IDENTITY, bias=bias_kv[:, t : t + 1], scale=1.0
+                    )
+            k_of[i] = k_sb
+
+        def project_values_and_bind(i):
+            product = bind_pool.tile([P, 4, BLOCK], BF16)
+            for u in range(2):
+                bank = project("Wbv", ("values", i), u)
+                for e in range(2):
+                    t = 2 * u + e
+                    nc.vector.scalar_tensor_tensor(
+                        out=product[:, t, :],
+                        in0=bank[:, BLOCK * e : BLOCK * (e + 1)],
+                        scalar=bias_kv[:, 4 + t : 5 + t],
+                        in1=k_of[i][:, t, :],
+                        op0=ADD,
+                        op1=MULT,
+                    )
+            product_grouped = bind_pool.tile([P, BLOCK, 4], BF16, align_bytes=64)
+            nc.scalar.copy(out=product_grouped[:], in_=product[:].rearrange("p t n -> p n t"))
+            block_codes = bind_pool.tile([P, BLOCK], U32, align_bytes=64)
+            block_scales = bind_pool.tile([P, BLOCK], U8, align_bytes=64)
+            nc.vector.quantize_mx(
+                out=block_codes[:].bitcast(FP8X4), scales=block_scales[:], in_=product_grouped[:].rearrange("p n t -> p (n t)")
+            )
+            bound_codes[i] = block_codes
+            bound_scales[i] = block_scales
+
+        def combine(i, m):
+            result = result_pool.tile([P, D], F32)
+            tokens = slice(P * m, P * (m + 1))
+            for n in range(D // BANK):
+                half = ("Wbc", n // 2)
+                cols = slice(BANK * (n % 2), BANK * (n % 2 + 1))
+                bank = psum.tile([P, BANK], F32, tag="bank")
+                nc.tensor.matmul_mx(
+                    out=bank[:],
+                    lhsT=bound_codes[i][:, tokens].bitcast(FP8X4),
+                    lhsT_scale=bound_scales[i][:, tokens],
+                    rhs=codes[half][:, cols].bitcast(FP8X4),
+                    rhs_scale=scales[half][:, cols],
+                    start=True,
+                    stop=True,
+                )
+                nc.vector.tensor_tensor(
+                    out=result[:, BANK * n : BANK * (n + 1)], in0=bank[:], in1=bias_c[:, BANK * n : BANK * (n + 1)], op=ADD
+                )
+            nc.sync.dma_start(out=out_rows[i, :, m, :], in_=result[:])
+
+        with tc.manual_schedule():
+            for slab in load_order[:2]:
+                load(slab)
+
+            ident = const.tile([P, P], F32)
+            make_identity(nc, ident[:])
+            ones = const.tile([P, P], BF16)
+            nc.vector.memset(ones[:], 1.0)
+            table_warmer = const.tile([P, 1], F32)
+            nc.scalar.activation(out=table_warmer[:], in_=ones[:, 0:1], func=IDENTITY)
+            bbc_row = const.tile([P, D], BF16)
+            nc.vector.memset(bbc_row[:], 0.0)
+            nc.sync.dma_start(out=bbc_row[0:1, :], in_=bbc.rearrange("(o d) -> o d", o=1))
+            bias_rows = const.tile([P, 2 * P], BF16)
+            nc.vector.memset(bias_rows[:], 0.0)
+            nc.sync.dma_start(out=bias_rows[0:2, :], in_=bbk.rearrange("(u w) -> u w", u=2))
+            nc.sync.dma_start(out=bias_rows[2:4, :], in_=bbv.rearrange("(u w) -> u w", u=2))
+
+            for slab in load_order[2:RAW_BUFS]:
+                load(slab)
+
+            for slab in load_order[:4]:
+                turn(slab)
+                quantise(slab)
+
+            bias_c = const.tile([P, D], F32)
+            for n in range(D // BANK):
+                bank = psum.tile([P, BANK], F32, tag="bank")
+                nc.tensor.matmul(out=bank[:], lhsT=ones[:], rhs=bbc_row[:, BANK * n : BANK * (n + 1)], start=True, stop=True)
+                nc.vector.tensor_copy(out=bias_c[:, BANK * n : BANK * (n + 1)], in_=bank[:])
+            bank = psum.tile([P, BANK], F32, tag="bank")
+            nc.tensor.transpose(bank[:, 0:P], bias_rows[:].bitcast(F32), ident[:])
+            bias_kv = const.tile([P, 8], F32)
+            nc.vector.tensor_copy(out=bias_kv[:], in_=bank[:, 0:4].bitcast(BF16))
+
+            for i in range(BLOCKS + 2):
+                if i < BLOCKS:
+                    turn(("keys", i))
+                if 1 <= i <= BLOCKS:
+                    quantise(("values", i - 1))
+                if i >= 2:
+                    combine(i - 2, 1)
+                if i < BLOCKS:
+                    quantise(("keys", i))
+                if 1 <= i <= BLOCKS:
+                    project_values_and_bind(i - 1)
+                if i < BLOCKS:
+                    turn(("values", i))
+                    project_keys(i)
+                if 1 <= i <= BLOCKS:
+                    combine(i - 1, 0)
+                if i == 0:
+                    for slab in (("Wbc", 0), ("Wbc", 1)):
+                        turn(slab)
+                        quantise(slab)

@@ -22,6 +22,8 @@ BLOCKS = TOKENS // BLOCK
 SLAB = 4096
 SLAB_BANKS = 4
 RAW_BUFS = 8
+EARLY_BLOCKS = 2
+LAG = 2
 
 FLOPS = 2 * TOKENS * (D * BD + D * BD + BD * D)
 
@@ -35,23 +37,27 @@ def tile_learnedbindingmemory_pa_kernel(tc, keys, values, Wbk, bbk, Wbv, bbv, Wb
         "Wbv": Wbv,
         "Wbc": Wbc,
     }
+    weight_of = {"keys": "Wbk", "values": "Wbv"}
     out_rows = out.flatten_outer_dims().rearrange("(i p m) d -> i p m d", p=P, m=2)
 
-    load_order = [("Wbk", 0), ("Wbk", 1), ("Wbv", 0), ("Wbv", 1), ("keys", 0), ("values", 0), ("Wbc", 0), ("Wbc", 1)]
-    for i in range(1, BLOCKS):
-        load_order.extend([("keys", i), ("values", i)])
+    load_order = [("Wbk", 0), ("keys", 0), ("Wbk", 1), ("keys", 1), ("Wbv", 0), ("values", 0), ("Wbv", 1), ("values", 1)]
+    load_order.extend([("Wbc", 0), ("Wbc", 1), ("keys", 2), ("values", 2), ("keys", 3), ("values", 3)])
 
     with tc.tile_pool(name="const", bufs=1) as const, tc.tile_pool(name="raw", bufs=RAW_BUFS) as raw_pool, tc.tile_pool(
         name="grouped", bufs=3
     ) as grouped_pool, tc.tile_pool(name="weights", bufs=1) as weight_pool, tc.tile_pool(
         name="stream", bufs=3
     ) as stream_pool, tc.tile_pool(name="bind", bufs=2) as bind_pool, tc.tile_pool(
-        name="result", bufs=4
-    ) as result_pool, tc.psum_pool(name="psum", bufs=8) as psum:
+        name="bound", bufs=3
+    ) as bound_pool, tc.tile_pool(name="result", bufs=3) as result_pool, tc.psum_pool(name="psum", bufs=8) as psum:
         words = {}
         grouped = {}
         codes = {}
         scales = {}
+        k_of = {}
+        product_of = {}
+        bound_codes = {}
+        bound_scales = {}
 
         def load(slab):
             name, index = slab
@@ -75,27 +81,26 @@ def tile_learnedbindingmemory_pa_kernel(tc, keys, values, Wbk, bbk, Wbv, bbv, Wb
                 for u in range(2):
                     for c in range(2):
                         nc.tensor.transpose(bank[:, (2 * u + c) * P : (2 * u + c + 1) * P], words[slab][:, j, u, c, :], ident[:])
-                pairs_in = bank[:].rearrange("p (u r) -> p r u", u=2)
-                pairs_out = turned_words[:, BANK * j : BANK * (j + 1)].rearrange("p (r u) -> p r u", u=2)
-                if slab[0] in ("Wbk", "Wbv", "Wbc") and j == SLAB_BANKS - 1:
-                    nc.vector.tensor_copy(out=pairs_out, in_=pairs_in)
-                else:
-                    nc.scalar.copy(out=pairs_out, in_=pairs_in)
+                nc.scalar.copy(
+                    out=turned_words[:, BANK * j : BANK * (j + 1)].rearrange("p (r u) -> p r u", u=2),
+                    in_=bank[:].rearrange("p (u r) -> p r u", u=2),
+                )
             grouped[slab] = turned
             following = load_order.index(slab) + RAW_BUFS
             if following < len(load_order):
                 load(load_order[following])
 
         def quantise(slab):
-            pool = weight_pool if slab[0] in ("Wbk", "Wbv", "Wbc") else stream_pool
-            label = "%s%d" % slab if pool is weight_pool else "stream"
+            pool = stream_pool if slab[0] in weight_of else weight_pool
+            label = "stream" if slab[0] in weight_of else "%s%d" % slab
             slab_codes = pool.tile([P, SLAB // 4], U32, align_bytes=64, name="codes_" + label)
             slab_scales = pool.tile([P, SLAB // 4], U8, align_bytes=64, name="scales_" + label)
             nc.vector.quantize_mx(out=slab_codes[:].bitcast(FP8X4), scales=slab_scales[:], in_=grouped[slab][:])
             codes[slab] = slab_codes
             scales[slab] = slab_scales
 
-        def project(weight, stream, u):
+        def project(stream, i, u):
+            weight = (weight_of[stream], u)
             bank = psum.tile([P, BANK], F32, tag="bank")
             for e in range(2):
                 for g in range(PASSES):
@@ -103,74 +108,67 @@ def tile_learnedbindingmemory_pa_kernel(tc, keys, values, Wbk, bbk, Wbv, bbv, Wb
                     s_cols = slice(BLOCK * g, BLOCK * (g + 1))
                     nc.tensor.matmul_mx(
                         out=bank[:, BLOCK * e : BLOCK * (e + 1)],
-                        lhsT=codes[(weight, u)][:, w_cols].bitcast(FP8X4),
-                        lhsT_scale=scales[(weight, u)][:, w_cols],
-                        rhs=codes[stream][:, s_cols].bitcast(FP8X4),
-                        rhs_scale=scales[stream][:, s_cols],
+                        lhsT=codes[weight][:, w_cols].bitcast(FP8X4),
+                        lhsT_scale=scales[weight][:, w_cols],
+                        rhs=codes[(stream, i)][:, s_cols].bitcast(FP8X4),
+                        rhs_scale=scales[(stream, i)][:, s_cols],
                         start=(g == 0),
                         stop=(g == PASSES - 1),
                     )
-            return bank
-
-        k_of = {}
-        bound_codes = {}
-        bound_scales = {}
-
-        def project_keys(i):
-            k_sb = bind_pool.tile([P, 4, BLOCK], F32)
-            for u in range(2):
-                bank = project("Wbk", ("keys", i), u)
-                for e in range(2):
-                    t = 2 * u + e
-                    nc.scalar.activation(
-                        out=k_sb[:, t, :], in_=bank[:, BLOCK * e : BLOCK * (e + 1)], func=IDENTITY, bias=bias_kv[:, t : t + 1], scale=1.0
-                    )
-            k_of[i] = k_sb
-
-        def project_values_and_bind(i):
-            product = bind_pool.tile([P, 4, BLOCK], BF16)
-            for u in range(2):
-                bank = project("Wbv", ("values", i), u)
-                for e in range(2):
-                    t = 2 * u + e
+            if u == 0 and stream == "keys":
+                k_sb = bind_pool.tile([P, 4, BLOCK], F32)
+                k_of[i] = k_sb
+            if u == 0 and stream == "values":
+                product = bind_pool.tile([P, 4, BLOCK], BF16)
+                product_of[i] = product
+            for e in range(2):
+                t = 2 * u + e
+                half_bank = bank[:, BLOCK * e : BLOCK * (e + 1)]
+                if stream == "keys":
+                    nc.scalar.activation(out=k_of[i][:, t, :], in_=half_bank, func=IDENTITY, bias=bias_kv[:, t : t + 1], scale=1.0)
+                else:
                     nc.vector.scalar_tensor_tensor(
-                        out=product[:, t, :],
-                        in0=bank[:, BLOCK * e : BLOCK * (e + 1)],
+                        out=product_of[i][:, t, :],
+                        in0=half_bank,
                         scalar=bias_kv[:, 4 + t : 5 + t],
                         in1=k_of[i][:, t, :],
                         op0=ADD,
                         op1=MULT,
                     )
-            product_grouped = bind_pool.tile([P, BLOCK, 4], BF16, align_bytes=64)
-            nc.scalar.copy(out=product_grouped[:], in_=product[:].rearrange("p t n -> p n t"))
-            block_codes = bind_pool.tile([P, BLOCK], U32, align_bytes=64)
-            block_scales = bind_pool.tile([P, BLOCK], U8, align_bytes=64)
-            nc.vector.quantize_mx(
-                out=block_codes[:].bitcast(FP8X4), scales=block_scales[:], in_=product_grouped[:].rearrange("p n t -> p (n t)")
-            )
-            bound_codes[i] = block_codes
-            bound_scales[i] = block_scales
+            if u == 1 and stream == "values":
+                product_grouped = bind_pool.tile([P, BLOCK, 4], BF16, align_bytes=64)
+                nc.vector.tensor_copy(out=product_grouped[:], in_=product_of[i][:].rearrange("p t n -> p n t"))
+                block_codes = bound_pool.tile([P, BLOCK], U32, align_bytes=64)
+                block_scales = bound_pool.tile([P, BLOCK], U8, align_bytes=64)
+                nc.vector.quantize_mx(
+                    out=block_codes[:].bitcast(FP8X4),
+                    scales=block_scales[:],
+                    in_=product_grouped[:].rearrange("p n t -> p (n t)"),
+                )
+                bound_codes[i] = block_codes
+                bound_scales[i] = block_scales
 
         def combine(i, m):
             result = result_pool.tile([P, D], F32)
             tokens = slice(P * m, P * (m + 1))
-            for n in range(D // BANK):
-                half = ("Wbc", n // 2)
-                cols = slice(BANK * (n % 2), BANK * (n % 2 + 1))
-                bank = psum.tile([P, BANK], F32, tag="bank")
-                nc.tensor.matmul_mx(
-                    out=bank[:],
-                    lhsT=bound_codes[i][:, tokens].bitcast(FP8X4),
-                    lhsT_scale=bound_scales[i][:, tokens],
-                    rhs=codes[half][:, cols].bitcast(FP8X4),
-                    rhs_scale=scales[half][:, cols],
-                    start=True,
-                    stop=True,
-                )
-                nc.vector.tensor_tensor(
-                    out=result[:, BANK * n : BANK * (n + 1)], in0=bank[:], in1=bias_c[:, BANK * n : BANK * (n + 1)], op=ADD
-                )
-            nc.sync.dma_start(out=out_rows[i, :, m, :], in_=result[:])
+            for half in range(2):
+                for n in (2 * half, 2 * half + 1):
+                    cols = slice(BANK * (n % 2), BANK * (n % 2 + 1))
+                    bank = psum.tile([P, BANK], F32, tag="bank")
+                    nc.tensor.matmul_mx(
+                        out=bank[:],
+                        lhsT=bound_codes[i][:, tokens].bitcast(FP8X4),
+                        lhsT_scale=bound_scales[i][:, tokens],
+                        rhs=codes[("Wbc", half)][:, cols].bitcast(FP8X4),
+                        rhs_scale=scales[("Wbc", half)][:, cols],
+                        start=True,
+                        stop=True,
+                    )
+                    nc.vector.tensor_tensor(
+                        out=result[:, BANK * n : BANK * (n + 1)], in0=bank[:], in1=bias_c[:, BANK * n : BANK * (n + 1)], op=ADD
+                    )
+                stored = slice(2 * BANK * half, 2 * BANK * (half + 1))
+                nc.sync.dma_start(out=out_rows[i, :, m, stored], in_=result[:, stored])
 
         with tc.manual_schedule():
             for slab in load_order[:2]:
@@ -189,41 +187,38 @@ def tile_learnedbindingmemory_pa_kernel(tc, keys, values, Wbk, bbk, Wbv, bbv, Wb
             nc.vector.memset(bias_rows[:], 0.0)
             nc.sync.dma_start(out=bias_rows[0:2, :], in_=bbk.rearrange("(u w) -> u w", u=2))
             nc.sync.dma_start(out=bias_rows[2:4, :], in_=bbv.rearrange("(u w) -> u w", u=2))
+            bias_c = const.tile([P, D], F32)
+            bias_kv = const.tile([P, 8], F32)
 
             for slab in load_order[2:RAW_BUFS]:
                 load(slab)
 
-            for slab in load_order[:4]:
-                turn(slab)
-                quantise(slab)
+            early_banks = [(stream, i, u) for stream in ("keys", "values") for i in range(EARLY_BLOCKS) for u in (0, 1)]
+            first_early = load_order.index(("keys", 0)) + LAG
+            first_combine = load_order.index(("Wbc", 1)) + LAG
 
-            bias_c = const.tile([P, D], F32)
-            for n in range(D // BANK):
-                bank = psum.tile([P, BANK], F32, tag="bank")
-                nc.tensor.matmul(out=bank[:], lhsT=ones[:], rhs=bbc_row[:, BANK * n : BANK * (n + 1)], start=True, stop=True)
-                nc.vector.tensor_copy(out=bias_c[:, BANK * n : BANK * (n + 1)], in_=bank[:])
-            bank = psum.tile([P, BANK], F32, tag="bank")
-            nc.tensor.transpose(bank[:, 0:P], bias_rows[:].bitcast(F32), ident[:])
-            bias_kv = const.tile([P, 8], F32)
-            nc.vector.tensor_copy(out=bias_kv[:], in_=bank[:, 0:4].bitcast(BF16))
+            for step in range(first_combine + 2 * BLOCKS):
+                if step < len(load_order):
+                    turn(load_order[step])
+                if 1 <= step <= len(load_order):
+                    quantise(load_order[step - 1])
 
-            for i in range(BLOCKS + 2):
-                if i < BLOCKS:
-                    turn(("keys", i))
-                if 1 <= i <= BLOCKS:
-                    quantise(("values", i - 1))
-                if i >= 2:
-                    combine(i - 2, 1)
-                if i < BLOCKS:
-                    quantise(("keys", i))
-                if 1 <= i <= BLOCKS:
-                    project_values_and_bind(i - 1)
-                if i < BLOCKS:
-                    turn(("values", i))
-                    project_keys(i)
-                if 1 <= i <= BLOCKS:
-                    combine(i - 1, 0)
-                if i == 0:
-                    for slab in (("Wbc", 0), ("Wbc", 1)):
-                        turn(slab)
-                        quantise(slab)
+                if step == first_early - 1:
+                    for n in range(D // BANK):
+                        bank = psum.tile([P, BANK], F32, tag="bank")
+                        nc.tensor.matmul(out=bank[:], lhsT=ones[:], rhs=bbc_row[:, BANK * n : BANK * (n + 1)], start=True, stop=True)
+                        nc.vector.tensor_copy(out=bias_c[:, BANK * n : BANK * (n + 1)], in_=bank[:])
+                    bank = psum.tile([P, BANK], F32, tag="bank")
+                    nc.tensor.transpose(bank[:, 0:P], bias_rows[:].bitcast(F32), ident[:])
+                    nc.vector.tensor_copy(out=bias_kv[:], in_=bank[:, 0:4].bitcast(BF16))
+
+                if first_early <= step < first_early + len(early_banks):
+                    stream, i, u = early_banks[step - first_early]
+                    project(stream, i, u)
+                if LAG <= step < len(load_order) + LAG:
+                    name, index = load_order[step - LAG]
+                    if name in weight_of and index >= EARLY_BLOCKS:
+                        project(name, index, 0)
+                        project(name, index, 1)
+                if step >= first_combine:
+                    combine((step - first_combine) // 2, (step - first_combine) % 2)

@@ -164,9 +164,12 @@ def tile_learnedbindingmemory_pa_kernel(tc, keys, values, Wbk, bbk, Wbv, bbv, Wb
                         start=True,
                         stop=True,
                     )
-                    nc.vector.tensor_tensor(
-                        out=result[:, BANK * n : BANK * (n + 1)], in0=bank[:], in1=bias_c[:, BANK * n : BANK * (n + 1)], op=ADD
-                    )
+                    piece = slice(BANK * n, BANK * (n + 1))
+                    if n % 2 == 0:
+                        nc.vector.tensor_tensor(out=result[:, piece], in0=bank[:], in1=bias_c[:, piece], op=ADD)
+                    else:
+                        nc.scalar.copy(out=result[:, piece], in_=bank[:])
+                        nc.gpsimd.tensor_tensor(out=result[:, piece], in0=result[:, piece], in1=bias_c[:, piece], op=ADD)
                 stored = slice(2 * BANK * half, 2 * BANK * (half + 1))
                 nc.sync.dma_start(out=out_rows[i, :, m, stored], in_=result[:, stored])
 

@@ -151,6 +151,7 @@ def tile_learnedbindingmemory_pa_kernel(tc, keys, values, Wbk, bbk, Wbv, bbv, Wb
         def combine(i, m):
             result = result_pool.tile([P, D], F32)
             tokens = slice(P * m, P * (m + 1))
+            relieved = (0, 2) if i < EARLY_BLOCKS else (0,) if (i, m) != (BLOCKS - 1, 1) else ()
             for half in range(2):
                 for n in (2 * half, 2 * half + 1):
                     cols = slice(BANK * (n % 2), BANK * (n % 2 + 1))
@@ -165,11 +166,11 @@ def tile_learnedbindingmemory_pa_kernel(tc, keys, values, Wbk, bbk, Wbv, bbv, Wb
                         stop=True,
                     )
                     piece = slice(BANK * n, BANK * (n + 1))
-                    if n % 2 == 0:
-                        nc.vector.tensor_tensor(out=result[:, piece], in0=bank[:], in1=bias_c[:, piece], op=ADD)
-                    else:
+                    if n in relieved:
                         nc.scalar.copy(out=result[:, piece], in_=bank[:])
                         nc.gpsimd.tensor_tensor(out=result[:, piece], in0=result[:, piece], in1=bias_c[:, piece], op=ADD)
+                    else:
+                        nc.vector.tensor_tensor(out=result[:, piece], in0=bank[:], in1=bias_c[:, piece], op=ADD)
                 stored = slice(2 * BANK * half, 2 * BANK * (half + 1))
                 nc.sync.dma_start(out=out_rows[i, :, m, stored], in_=result[:, stored])
 
@@ -199,8 +200,10 @@ def tile_learnedbindingmemory_pa_kernel(tc, keys, values, Wbk, bbk, Wbv, bbv, Wb
             early_banks = [(stream, i, u) for stream in ("keys", "values") for i in range(EARLY_BLOCKS) for u in (0, 1)]
             first_early = load_order.index(("keys", 0)) + LAG
             first_combine = load_order.index(("Wbc", 1)) + LAG
+            tiles = 2 * BLOCKS
+            combine_step = [first_combine + min(max(j - 1, 0), tiles - 3) for j in range(tiles)]
 
-            for step in range(first_combine + 2 * BLOCKS):
+            for step in range(combine_step[-1] + 1):
                 if step < len(load_order):
                     turn(load_order[step])
                 if 1 <= step <= len(load_order):
@@ -223,5 +226,6 @@ def tile_learnedbindingmemory_pa_kernel(tc, keys, values, Wbk, bbk, Wbv, bbv, Wb
                     if name in weight_of and index >= EARLY_BLOCKS:
                         project(name, index, 0)
                         project(name, index, 1)
-                if step >= first_combine:
-                    combine((step - first_combine) // 2, (step - first_combine) % 2)
+                for j in range(tiles):
+                    if combine_step[j] == step:
+                        combine(j // 2, j % 2)

@@ -206,7 +206,7 @@ def tile_learnedbindingmemory_pa_kernel(tc, keys, values, Wbk, bbk, Wbv, bbv, Wb
             for step in range(combine_step[-1] + 1):
                 if step < len(load_order):
                     turn(load_order[step])
-                if 1 <= step <= len(load_order):
+                if 1 <= step < len(load_order):
                     quantise(load_order[step - 1])
 
                 if step == first_early - 1:
@@ -226,6 +226,8 @@ def tile_learnedbindingmemory_pa_kernel(tc, keys, values, Wbk, bbk, Wbv, bbv, Wb
                     if name in weight_of and index >= EARLY_BLOCKS:
                         project(name, index, 0)
                         project(name, index, 1)
+                if step == len(load_order) - 1:
+                    quantise(load_order[step])
                 for j in range(tiles):
                     if combine_step[j] == step:
                         combine(j // 2, j % 2)

import concourse.mybir as mybir
from concourse.masks import make_identity

F32 = mybir.dt.float32
BF16 = mybir.dt.bfloat16
U32 = mybir.dt.uint32
U8 = mybir.dt.uint8
FP8X4 = mybir.dt.float8_e4m3fn_x4
ADD = mybir.AluOpType.add
MULT = mybir.AluOpType.mult
IDENTITY = mybir.ActivationFunctionType.Identity

P = 128
TOKENS = 1024
D = 2048
BD = 512
K_PASS = 512
PASSES = D // K_PASS
BANK = 512
BLOCK = 256
BLOCKS = TOKENS // BLOCK
SLAB = 4096
SLAB_BANKS = 4
RAW_BUFS = 8
EARLY_BLOCKS = 2
LAG = 2

FLOPS = 2 * TOKENS * (D * BD + D * BD + BD * D)


def tile_learnedbindingmemory_pa_kernel(tc, keys, values, Wbk, bbk, Wbv, bbv, Wbc, bbc, out):
    nc = tc.nc
    source = {
        "keys": keys.flatten_outer_dims(),
        "values": values.flatten_outer_dims(),
        "Wbk": Wbk,
        "Wbv": Wbv,
        "Wbc": Wbc,
    }
    weight_of = {"keys": "Wbk", "values": "Wbv"}
    out_rows = out.flatten_outer_dims().rearrange("(i p m) d -> i p m d", p=P, m=2)

    load_order = [("Wbk", 0), ("keys", 0), ("Wbk", 1), ("keys", 1), ("Wbv", 0), ("values", 0), ("Wbv", 1), ("values", 1)]
    load_order.extend([("Wbc", 0), ("Wbc", 1), ("keys", 2), ("values", 2), ("keys", 3), ("values", 3)])

    with tc.tile_pool(name="const", bufs=1) as const, tc.tile_pool(name="raw", bufs=RAW_BUFS) as raw_pool, tc.tile_pool(
        name="grouped", bufs=3
    ) as grouped_pool, tc.tile_pool(name="weights", bufs=1) as weight_pool, tc.tile_pool(
        name="stream", bufs=3
    ) as stream_pool, tc.tile_pool(name="bind", bufs=2) as bind_pool, tc.tile_pool(
        name="bound", bufs=3
    ) as bound_pool, tc.tile_pool(name="result", bufs=3) as result_pool, tc.psum_pool(name="psum", bufs=8) as psum:
        words = {}
        grouped = {}
        codes = {}
        scales = {}
        k_of = {}
        product_of = {}
        bound_codes = {}
        bound_scales = {}

        def load(slab):
            name, index = slab
            raw = raw_pool.tile([P, SLAB], BF16)
            if name == "Wbc":
                rows = source[name][1024 * index : 1024 * (index + 1), :]
                nc.sync.dma_start(
                    out=raw[:].rearrange("p (c k) -> p c k", c=8), in_=rows.rearrange("(c p) k -> p c k", p=P)
                )
                words[slab] = raw[:].bitcast(F32).rearrange("p (j c u w) -> p j u c w", j=SLAB_BANKS, c=2, u=2)
            else:
                rows = source[name][256 * index : 256 * (index + 1), :]
                nc.sync.dma_start(out=raw[:], in_=rows.rearrange("(p c) d -> p (c d)", c=2))
                words[slab] = raw[:].bitcast(F32).rearrange("p (c g u w) -> p g u c w", c=2, g=PASSES, u=2)

        def turn(slab):
            turned = grouped_pool.tile([P, SLAB], BF16, align_bytes=64)
            turned_words = turned[:].bitcast(F32)
            for j in range(SLAB_BANKS):
                bank = psum.tile([P, BANK], F32, tag="bank")
                for u in range(2):
                    for c in range(2):
                        nc.tensor.transpose(bank[:, (2 * u + c) * P : (2 * u + c + 1) * P], words[slab][:, j, u, c, :], ident[:])
                nc.scalar.copy(
                    out=turned_words[:, BANK * j : BANK * (j + 1)].rearrange("p (r u) -> p r u", u=2),
                    in_=bank[:].rearrange("p (u r) -> p r u", u=2),
                )
            grouped[slab] = turned
            following = load_order.index(slab) + RAW_BUFS
            if following < len(load_order):
                load(load_order[following])

        def quantise(slab):
            pool = stream_pool if slab[0] in weight_of else weight_pool
            label = "stream" if slab[0] in weight_of else "%s%d" % slab
            slab_codes = pool.tile([P, SLAB // 4], U32, align_bytes=64, name="codes_" + label)
            slab_scales = pool.tile([P, SLAB // 4], U8, align_bytes=64, name="scales_" + label)
            nc.vector.quantize_mx(out=slab_codes[:].bitcast(FP8X4), scales=slab_scales[:], in_=grouped[slab][:])
            codes[slab] = slab_codes
            scales[slab] = slab_scales

        def project(stream, i, u):
            weight = (weight_of[stream], u)
            bank = psum.tile([P, BANK], F32, tag="bank")
            for e in range(2):
                for g in range(PASSES):
                    w_cols = slice(BLOCK * g + P * e, BLOCK * g + P * (e + 1))
                    s_cols = slice(BLOCK * g, BLOCK * (g + 1))
                    nc.tensor.matmul_mx(
                        out=bank[:, BLOCK * e : BLOCK * (e + 1)],
                        lhsT=codes[weight][:, w_cols].bitcast(FP8X4),
                        lhsT_scale=scales[weight][:, w_cols],
                        rhs=codes[(stream, i)][:, s_cols].bitcast(FP8X4),
                        rhs_scale=scales[(stream, i)][:, s_cols],
                        start=(g == 0),
                        stop=(g == PASSES - 1),
                    )
            if u == 0 and stream == "keys":
                k_sb = bind_pool.tile([P, 4, BLOCK], F32)
                k_of[i] = k_sb
            if u == 0 and stream == "values":
                product = bind_pool.tile([P, 4, BLOCK], BF16)
                product_of[i] = product
            for e in range(2):
                t = 2 * u + e
                half_bank = bank[:, BLOCK * e : BLOCK * (e + 1)]
                if stream == "keys":
                    nc.scalar.activation(out=k_of[i][:, t, :], in_=half_bank, func=IDENTITY, bias=bias_kv[:, t : t + 1], scale=1.0)
                else:
                    nc.vector.scalar_tensor_tensor(
                        out=product_of[i][:, t, :],
                        in0=half_bank,
                        scalar=bias_kv[:, 4 + t : 5 + t],
                        in1=k_of[i][:, t, :],
                        op0=ADD,
                        op1=MULT,
                    )
            if u == 1 and stream == "values":
                product_grouped = bind_pool.tile([P, BLOCK, 4], BF16, align_bytes=64)
                nc.vector.tensor_copy(out=product_grouped[:], in_=product_of[i][:].rearrange("p t n -> p n t"))
                block_codes = bound_pool.tile([P, BLOCK], U32, align_bytes=64)
                block_scales = bound_pool.tile([P, BLOCK], U8, align_bytes=64)
                nc.vector.quantize_mx(
                    out=block_codes[:].bitcast(FP8X4),
                    scales=block_scales[:],
                    in_=product_grouped[:].rearrange("p n t -> p (n t)"),
                )
                bound_codes[i] = block_codes
                bound_scales[i] = block_scales

        def combine(i, m):
            result = result_pool.tile([P, D], F32)
            tokens = slice(P * m, P * (m + 1))
            relieved = (0, 2) if i < EARLY_BLOCKS else (0,) if (i, m) != (BLOCKS - 1, 1) else ()
            for half in range(2):
                for n in (2 * half, 2 * half + 1):
                    cols = slice(BANK * (n % 2), BANK * (n % 2 + 1))
                    bank = psum.tile([P, BANK], F32, tag="bank")
                    nc.tensor.matmul_mx(
                        out=bank[:],
                        lhsT=bound_codes[i][:, tokens].bitcast(FP8X4),
                        lhsT_scale=bound_scales[i][:, tokens],
                        rhs=codes[("Wbc", half)][:, cols].bitcast(FP8X4),
                        rhs_scale=scales[("Wbc", half)][:, cols],
                        start=True,
                        stop=True,
                    )
                    piece = slice(BANK * n, BANK * (n + 1))
                    if n in relieved:
                        nc.scalar.copy(out=result[:, piece], in_=bank[:])
                        nc.gpsimd.tensor_tensor(out=result[:, piece], in0=result[:, piece], in1=bias_c[:, piece], op=ADD)
                    else:
                        nc.vector.tensor_tensor(out=result[:, piece], in0=bank[:], in1=bias_c[:, piece], op=ADD)
                stored = slice(2 * BANK * half, 2 * BANK * (half + 1))
                nc.sync.dma_start(out=out_rows[i, :, m, stored], in_=result[:, stored])

        with tc.manual_schedule():
            for slab in load_order[:2]:
                load(slab)

            ident = const.tile([P, P], F32)
            make_identity(nc, ident[:])
            ones = const.tile([P, P], BF16)
            nc.vector.memset(ones[:], 1.0)
            table_warmer = const.tile([P, 1], F32)
            nc.scalar.activation(out=table_warmer[:], in_=ones[:, 0:1], func=IDENTITY)
            bbc_row = const.tile([P, D], BF16)
            nc.vector.memset(bbc_row[:], 0.0)
            nc.sync.dma_start(out=bbc_row[0:1, :], in_=bbc.rearrange("(o d) -> o d", o=1))
            bias_rows = const.tile([P, 2 * P], BF16)
            nc.vector.memset(bias_rows[:], 0.0)
            nc.sync.dma_start(out=bias_rows[0:2, :], in_=bbk.rearrange("(u w) -> u w", u=2))
            nc.sync.dma_start(out=bias_rows[2:4, :], in_=bbv.rearrange("(u w) -> u w", u=2))
            bias_c = const.tile([P, D], F32)
            bias_kv = const.tile([P, 8], F32)

            for slab in load_order[2:RAW_BUFS]:
                load(slab)

            early_banks = [(stream, i, u) for stream in ("keys", "values") for i in range(EARLY_BLOCKS) for u in (0, 1)]
            first_early = load_order.index(("keys", 0)) + LAG
            first_combine = load_order.index(("Wbc", 1)) + LAG
            tiles = 2 * BLOCKS
            combine_step = [first_combine + min(max(j - 1, 0), tiles - 3) for j in range(tiles)]

            for step in range(combine_step[-1] + 1):
                if step < len(load_order):
                    turn(load_order[step])
                if 1 <= step < len(load_order):
                    quantise(load_order[step - 1])

                if step == first_early - 1:
                    for n in range(D // BANK):
                        bank = psum.tile([P, BANK], F32, tag="bank")
                        nc.tensor.matmul(out=bank[:], lhsT=ones[:], rhs=bbc_row[:, BANK * n : BANK * (n + 1)], start=True, stop=True)
                        nc.vector.tensor_copy(out=bias_c[:, BANK * n : BANK * (n + 1)], in_=bank[:])
                    bank = psum.tile([P, BANK], F32, tag="bank")
                    nc.tensor.transpose(bank[:, 0:P], bias_rows[:].bitcast(F32), ident[:])
                    nc.vector.tensor_copy(out=bias_kv[:], in_=bank[:, 0:4].bitcast(BF16))

                if first_early <= step < first_early + len(early_banks):
                    stream, i, u = early_banks[step - first_early]
                    project(stream, i, u)
                if LAG <= step < len(load_order) + LAG:
                    name, index = load_order[step - LAG]
                    if name in weight_of and index >= EARLY_BLOCKS:
                        project(name, index, 0)
                        project(name, index, 1)
                if step == len(load_order) - 1:
                    quantise(load_order[step])
                for j in range(tiles):
                    if combine_step[j] == step:
                        combine(j // 2, j % 2)
